import numpy as np
import ml_dtypes


def mxq(x, axis, fmt="e4m3"):
    dtype, down = {"e4m3": (ml_dtypes.float8_e4m3fn, 7), "e5m2": (ml_dtypes.float8_e5m2, 14)}[fmt]
    v = np.moveaxis(np.asarray(x, np.float32).astype(ml_dtypes.bfloat16).astype(np.float64), axis, -1)
    blocks = v.reshape(v.shape[:-1] + (-1, 32))
    amax = np.abs(blocks).max(-1, keepdims=True)
    byte = np.maximum(np.where(amax > 0, np.frexp(amax)[1] - 1 + 127, 0) - down, 1)
    scale = np.exp2(byte - 127.0)
    codes = (blocks / scale).astype(np.float32).astype(dtype).astype(np.float64)
    return np.moveaxis((codes * scale).reshape(v.shape), -1, axis)


WIDE = False


def mx_kscale(k):
    if not WIDE:
        return np.ones(k)
    levels = np.array([10, -10, 5, -5, 0])
    if k % 512:
        return np.exp2(np.random.permutation(np.resize(levels, k // 32))).repeat(32)
    a = np.empty((k // 512, 16))
    for p in range(k // 512):
        a[p, :8] = np.random.permutation(np.resize(levels, 8))
        for g in range(8):
            far = levels[np.abs(levels - a[p, g]) >= 10]
            a[p, g + 8] = far[np.random.randint(len(far))]
    return np.exp2(a.ravel()).repeat(32)


BF16 = ml_dtypes.bfloat16


def bf(x):
    return np.asarray(x, np.float32).astype(BF16)


def f64(x):
    return np.asarray(x).astype(np.float64)


E2M1 = np.array([0.0, 0.5, 1.0, 1.5, 2.0, 3.0, 4.0, 6.0, -0.0, -0.5, -1.0, -1.5, -2.0, -3.0, -4.0, -6.0])


def pack_weight(w, fmt):
    k, n = w.shape
    w = f64(bf(w)).reshape(k // 32, 32, n)
    amax = np.abs(w).max(1)
    if fmt == "e4m3":
        byte = np.frexp(amax)[1] - 1 + 127 - 7
    else:
        mant, ex = np.frexp(amax / 6.0)
        byte = np.where(mant > 0.5, ex, ex - 1) + 127
    byte = np.clip(np.where(amax > 0, byte, 1), 1, 254)
    scaled = (w * np.exp2(127.0 - byte)[:, None, :]).reshape(k, n).astype(np.float32)
    by_word = np.ascontiguousarray(scaled.reshape(k // 512, 128, 4, n).transpose(0, 1, 3, 2))
    if fmt == "e4m3":
        words = by_word.astype(ml_dtypes.float8_e4m3fn).view(np.uint8)
    else:
        c = by_word.astype(ml_dtypes.float4_e2m1fn).view(np.uint8) & 0xF
        words = c[..., 0::2] | (c[..., 1::2] << 4)
    return np.ascontiguousarray(words), np.ascontiguousarray(byte.astype(np.uint8).reshape(k // 512, 16, n))


def unpack_weight(words, scales, fmt):
    g, p, n, _ = words.shape
    if fmt == "e4m3":
        vals = np.ascontiguousarray(words).view(ml_dtypes.float8_e4m3fn).astype(np.float64)
    else:
        nib = np.empty((g, p, n, 4), np.uint8)
        nib[..., 0::2] = words & 0xF
        nib[..., 1::2] = words >> 4
        vals = E2M1[nib]
    vals = vals * np.repeat(np.exp2(scales.astype(np.float64) - 127.0), 8, axis=1)[..., None]
    return vals.transpose(0, 1, 3, 2).reshape(g * 512, n)


N, T, D, B0, C, P0, V1, P1, V2 = 2, 512, 1024, 2046, 2, 512, 2048, 512, 1024
MU = 0.25
SIG = 2.0


def softmax(v):
    e = np.exp(v - v.max(-1, keepdims=True))
    return e / e.sum(-1, keepdims=True)


def draw0():
    s, t = mx_kscale(D), mx_kscale(P0)
    hw = np.random.standard_normal((D, B0 + C)) * SIG / np.sqrt(D)
    hw[:, B0:] = hw[:, B0:] / SIG + (np.log(B0) + 0.5 * SIG * SIG) / (MU * D)
    x = bf((np.random.standard_normal((N, T, D)) + MU) * s)
    hw_words, hw_scales = pack_weight(hw / s[:, None], "e4m3")
    tp_words, tp_scales = pack_weight(np.random.standard_normal((D, P0)) / np.sqrt(D) / s[:, None] * t, "e4m3")
    tw_words, tw_scales = pack_weight(np.random.standard_normal((P0, V1)) * SIG / np.sqrt(P0) / t[:, None], "e4m3")
    return {"x": x,
            "head_weight_words": hw_words, "head_weight_scales": hw_scales,
            "tail_proj_0_words": tp_words, "tail_proj_0_scales": tp_scales,
            "tail_w_0_words": tw_words, "tail_w_0_scales": tw_scales}


def core(x, head_weight_words, head_weight_scales, tail_proj_0_words, tail_proj_0_scales, tail_w_0_words, tail_w_0_scales):
    xq = mxq(f64(x), 2, "e4m3")
    head_sm = softmax(xq @ unpack_weight(head_weight_words, head_weight_scales, "e4m3"))
    h = xq @ unpack_weight(tail_proj_0_words, tail_proj_0_scales, "e4m3")
    tail_sm = softmax(mxq(h, 2, "e4m3") @ unpack_weight(tail_w_0_words, tail_w_0_scales, "e4m3"))
    probs = np.concatenate([head_sm[..., :B0], tail_sm * head_sm[..., B0:B0 + 1]], axis=-1)
    return probs, head_sm[..., B0 + 1:B0 + C]


def e4m3fn_bytes(y):
    return np.clip(np.asarray(y, np.float64), -448.0, 448.0).astype(np.float32).astype(ml_dtypes.float8_e4m3fn).view(np.uint8)


def e4m3fn_values(b):
    return np.asarray(b, np.uint8).view(ml_dtypes.float8_e4m3fn).astype(np.float64)


def setup_inputs():
    d = draw0()
    x0 = np.asarray(d['x']).astype(np.float64)
    s = (np.max(np.abs(x0), axis=(0, 1), keepdims=True) / 448.0).astype(np.float32)
    out = {}
    for k, v in d.items():
        if k == 'x':
            out['x_bytes'] = e4m3fn_bytes(x0 / s.astype(np.float64))
            out['x_scale'] = s
        else:
            out[k] = v
    return out


def reference(x_bytes, x_scale, head_weight_words, head_weight_scales, tail_proj_0_words, tail_proj_0_scales, tail_w_0_words, tail_w_0_scales):
    return core(e4m3fn_values(x_bytes) * x_scale.astype(np.float64), head_weight_words, head_weight_scales, tail_proj_0_words, tail_proj_0_scales, tail_w_0_words, tail_w_0_scales)

@@ -1,0 +1,377 @@
+from contextlib import ExitStack
+
+import concourse.mybir as mybir
+from concourse.masks import make_identity
+
+F32 = mybir.dt.float32
+BF16 = mybir.dt.bfloat16
+I32 = mybir.dt.int32
+U8 = mybir.dt.uint8
+FP8 = mybir.dt.float8_e4m3fn
+FP8X4 = mybir.dt.float8_e4m3fn_x4
+ALU = mybir.AluOpType
+ACT = mybir.ActivationFunctionType
+AX = mybir.AxisListType
+
+P = 128
+NTOK = 1024
+D = 1024
+NH = 2048
+HEAD_OUT = 2046
+PROJ = 512
+NT = 2048
+ROW = HEAD_OUT + NT
+TILES = NTOK // P
+BANK = 512
+NB = NH // BANK
+LEAD = 4
+
+NAMES = ["cast", "xt", "p0", "p1", "xq", "hm", "hc", "hq", "sum", "recip", "sumE", "recE"]
+PLAN = {"cast": (4, 9), "xt": (2, 1), "p0": (2, 11), "p1": (1, 0), "xq": (1, 3), "hm": (2, 0), "hc": (2, 10), "hq": (1, 2), "sum": (-2, 0), "recip": (-2, 3), "sumE": (-1, 12), "recE": (-2, 4)}
+CAST = "vsssssss"
+EARLY = 12
+VSHARE = {13: 1024, 14: 1024}
+G = D // 512
+
+FLOPS = 2 * NTOK * (D * NH + D * PROJ + PROJ * NT)
+
+
+def tile_adaptiveinputsoftmax_pa_w8_kernel(
+    tc, x_bytes, x_scale, hw_words, hw_scales, tp_words, tp_scales, tw_words, tw_scales, probs, other
+):
+    nc = tc.nc
+
+    with ExitStack() as ctx:
+        keep = ctx.enter_context(tc.tile_pool(name="keep", bufs=1))
+        work = ctx.enter_context(tc.tile_pool(name="work", bufs=2))
+        work3 = ctx.enter_context(tc.tile_pool(name="work3", bufs=3))
+        work5 = ctx.enter_context(tc.tile_pool(name="work5", bufs=5))
+        epool = ctx.enter_context(tc.tile_pool(name="epool", bufs=4))
+        stat = ctx.enter_context(tc.tile_pool(name="stat", bufs=5))
+        logits = ctx.enter_context(tc.psum_pool(name="logits", bufs=7))
+        misc = ctx.enter_context(tc.psum_pool(name="misc", bufs=1))
+
+        xb = keep.tile([P, TILES, D], U8, align_bytes=64)
+        xs = keep.tile([P, G, 4], F32)
+        hw = keep.tile([P, NB, G, BANK], I32, align_bytes=64)
+        hs = keep.tile([P, NH], U8, align_bytes=64)
+        tpw = keep.tile([P, G, PROJ], I32, align_bytes=64)
+        tps = keep.tile([P, PROJ], U8, align_bytes=64)
+        tpw_perm = keep.tile([P, G, PROJ], I32, align_bytes=64)
+        tps_perm = keep.tile([P, PROJ], U8, align_bytes=64)
+        tw = keep.tile([P, NT], I32, align_bytes=64)
+        tws = keep.tile([P, NT], U8, align_bytes=64)
+        ident = keep.tile([P, P], F32)
+        outs = keep.tile([P, TILES * ROW], F32, align_bytes=64)
+        cluster = keep.tile([P, 2, TILES], F32)
+        warm = keep.tile([P, 1], F32)
+
+        x_view = x_bytes.flatten_outer_dims().rearrange("(p j) k -> p j k", j=TILES)
+        out_view = probs.flatten_outer_dims().rearrange("(p j) c -> p (j c)", j=TILES)
+        other_view = other.flatten_outer_dims().rearrange("(p j) c -> p (j c)", j=TILES)
+        hw_view = hw_words.rearrange("g p n t -> g p (n t)").bitcast(I32)
+        tp_view = tp_words.rearrange("g p n t -> g p (n t)").bitcast(I32)
+        tw_view = tw_words.rearrange("g p n t -> g p (n t)").bitcast(I32)
+
+        ctx.enter_context(tc.manual_schedule())
+
+        nc.vector.memset(hs[:].bitcast(I32), 0)
+        nc.vector.memset(warm[:], 0.0)
+        nc.vector.memset(tws[:].bitcast(I32), 0)
+        nc.vector.memset(tps[:].bitcast(I32), 0)
+        nc.scalar.activation(warm[:], warm[:], ACT.Exp)
+        make_identity(nc, ident[:])
+
+        def load_x(lo, hi):
+            nc.sync.dma_start(out=xb[:, lo:hi, :], in_=x_view[:, lo:hi, :])
+
+        def load_head(b):
+            nc.sync.dma_start(
+                out=hw[:, b, :, :], in_=hw_view[:, :, BANK * b : BANK * (b + 1)].rearrange("g p n -> p g n")
+            )
+
+        load_x(0, 1)
+        nc.sync.dma_start(out=xs[:], in_=x_scale.rearrange("a b (g p t) -> p (a b g) t", g=G, p=P, t=4))
+        load_x(1, 2)
+        for q in range(4):
+            nc.sync.dma_start(
+                out=hs[32 * q : 32 * q + 8, :].bitcast(I32), in_=hw_scales[:, 4 * q : 4 * q + 4, :].bitcast(I32)
+            )
+        load_head(0)
+        load_head(1)
+        load_x(2, 3)
+        load_head(2)
+        load_head(3)
+        for q in range(4):
+            nc.sync.dma_start(
+                out=tps[32 * q : 32 * q + 8, :].bitcast(I32), in_=tp_scales[:, 4 * q : 4 * q + 4, :].bitcast(I32)
+            )
+        nc.sync.dma_start(out=tpw[:], in_=tp_view.rearrange("g p n -> p g n"))
+        load_x(3, 4)
+        for q in range(4):
+            nc.sync.dma_start(
+                out=tws[32 * q : 32 * q + 4, :].bitcast(I32), in_=tw_scales[0, 4 * q : 4 * q + 4, :].bitcast(I32)
+            )
+        nc.sync.dma_start(out=tw[:], in_=tw_view[0])
+        load_x(4, 6)
+        load_x(6, 8)
+
+        nc.gpsimd.tensor_copy(
+            out=tps_perm[:].rearrange("p (t m) -> p t m", t=4), in_=tps[:].rearrange("p (m t) -> p t m", t=4)
+        )
+        for g in range(G):
+            nc.gpsimd.tensor_copy(
+                out=tpw_perm[:, g, :].rearrange("p (t m) -> p t m", t=4),
+                in_=tpw[:, g, :].rearrange("p (m t) -> p t m", t=4),
+            )
+
+        xbf, xt, xg, xc, xsc = {}, {}, {}, {}, {}
+        ht, hg, hc, hsc = {}, {}, {}, {}
+        lg, mx, nm, sm, rs, ex = {}, {}, {}, {}, {}, {}
+
+        def cast(j, eng):
+            src = xb[:, j, :].bitcast(FP8)
+            t = work3.tile([P, D], BF16, name="xbf", align_bytes=64)
+            xbf[j] = t
+            if eng is nc.scalar:
+                nc.scalar.copy(out=t[:], in_=src)
+            else:
+                eng.tensor_copy(out=t[:], in_=src)
+
+        def x_transpose(j):
+            t = misc.tile([P, BANK], F32, name="miscb")
+            xt[j] = t
+            words = xbf[j][:].bitcast(F32)
+            for g in range(G):
+                for u in range(2):
+                    nc.tensor.transpose(
+                        t[:, 128 * (2 * g + u) : 128 * (2 * g + u + 1)],
+                        words[:, 256 * g + u : 256 * (g + 1) : 2],
+                        ident[:],
+                    )
+
+        def x_product(j, g):
+            if g == 0:
+                t = work.tile([P, G, P, 4], BF16, name="xg", align_bytes=64)
+                xg[j] = t
+            nc.vector.tensor_tensor(
+                out=xg[j][:, g, :, :].rearrange("p r (u e) -> p r u e", e=2),
+                in0=xt[j][:, 256 * g : 256 * (g + 1)].bitcast(BF16).rearrange("p (u r e) -> p r u e", u=2, e=2),
+                in1=xs[:, g, :].rearrange("p (u e) -> p u e", e=2).unsqueeze(1).to_broadcast([P, P, 2, 2]),
+                op=ALU.mult,
+            )
+
+        def x_quantize(j):
+            c = work5.tile([P, G * P], I32, name="xc", align_bytes=64)
+            s = work5.tile([P, G * P], U8, name="xsc", align_bytes=64)
+            xc[j], xsc[j] = c, s
+            nc.vector.quantize_mx(
+                out=c[:].bitcast(FP8X4), scales=s[:], in_=xg[j][:].rearrange("p g r t -> p (g r t)")
+            )
+
+        def h_matmul(j):
+            t = misc.tile([P, BANK], F32, name="miscb")
+            ht[j] = t
+            for q in range(4):
+                for g in range(G):
+                    nc.tensor.matmul_mx(
+                        out=t[:, P * q : P * (q + 1)],
+                        lhsT=tpw_perm[:, g, P * q : P * (q + 1)].bitcast(FP8X4),
+                        lhsT_scale=tps_perm[4 * g :, P * q : P * (q + 1)],
+                        rhs=xc[j][:, P * g : P * (g + 1)].bitcast(FP8X4),
+                        rhs_scale=xsc[j][:, P * g : P * (g + 1)],
+                        start=(g == 0),
+                        stop=(g == G - 1),
+                    )
+
+        def h_copy(j):
+            t = work.tile([P, P, 4], BF16, name="hg", align_bytes=64)
+            hg[j] = t
+            nc.scalar.copy(out=t[:], in_=ht[j][:].rearrange("p (t n) -> p n t", t=4))
+
+        def h_quantize(j):
+            c = work3.tile([P, P], I32, name="hc", align_bytes=64)
+            s = work3.tile([P, P], U8, name="hsc", align_bytes=64)
+            hc[j], hsc[j] = c, s
+            nc.vector.quantize_mx(out=c[:].bitcast(FP8X4), scales=s[:], in_=hg[j][:].rearrange("p n t -> p (n t)"))
+
+        units = [("h", j) for j in range(LEAD)]
+        for j in range(LEAD, TILES):
+            units += [("t", j - LEAD), ("h", j)]
+        units += [("t", j) for j in range(TILES - LEAD, TILES)]
+        place = {unit: s for s, unit in enumerate(units)}
+
+        def logit_bank(s, b):
+            kind, j = units[s]
+            t = logits.tile([P, BANK], F32, name="lg")
+            lg[s, b] = t
+            cols = slice(BANK * b, BANK * (b + 1))
+            if kind == "h":
+                for g in range(G):
+                    nc.tensor.matmul_mx(
+                        out=t[:],
+                        lhsT=xc[j][:, P * g : P * (g + 1)].bitcast(FP8X4),
+                        lhsT_scale=xsc[j][:, P * g : P * (g + 1)],
+                        rhs=hw[:, b, g, :].bitcast(FP8X4),
+                        rhs_scale=hs[4 * g :, cols],
+                        start=(g == 0),
+                        stop=(g == G - 1),
+                    )
+            else:
+                nc.tensor.matmul_mx(
+                    out=t[:],
+                    lhsT=hc[j][:].bitcast(FP8X4),
+                    lhsT_scale=hsc[j][:],
+                    rhs=tw[:, cols].bitcast(FP8X4),
+                    rhs_scale=tws[:, cols],
+                    start=True,
+                    stop=True,
+                )
+
+        def bank_max(s, b):
+            if b == 0:
+                t = stat.tile([P, NB], F32, name="mx")
+                mx[s] = t
+            nc.vector.tensor_reduce(out=mx[s][:, b : b + 1], in_=lg[s, b][:], axis=AX.X, op=ALU.max)
+
+        def neg_max(s):
+            t = stat.tile([P, 1], F32, name="nm")
+            nm[s] = t
+            nc.vector.tensor_reduce(out=t[:], in_=mx[s][:], axis=AX.X, op=ALU.max, negate=True)
+
+        def bank_exp(s, b):
+            if b == 0:
+                t = stat.tile([P, NB], F32, name="sm")
+                sm[s] = t
+                e = epool.tile([P, NH], F32, name="ex", align_bytes=64)
+                ex[s] = e
+            nc.scalar.activation(
+                ex[s][:, BANK * b : BANK * (b + 1)],
+                lg[s, b][:],
+                ACT.Exp,
+                bias=nm[s][:],
+                scale=1.0,
+                accum_out=sm[s][:, b : b + 1],
+            )
+
+        def row_sum(s):
+            t = stat.tile([P, 2], F32, name="rs")
+            rs[s] = t
+            nc.vector.tensor_reduce(out=t[:, 0:1], in_=sm[s][:], axis=AX.X, op=ALU.add)
+
+        def row_recip(s):
+            nc.vector.reciprocal(out=rs[s][:, 1:2], in_=rs[s][:, 0:1])
+
+        def normalise(s, eng, lo, hi):
+            kind, j = units[s]
+            base = ROW * j + (0 if kind == "h" else HEAD_OUT)
+            eng.tensor_scalar(
+                out=outs[:, base + lo : base + hi],
+                in0=ex[s][:, lo:hi],
+                scalar1=rs[s][:, 1:2],
+                scalar2=1.0 if kind == "h" else cluster[:, 0, j : j + 1],
+                op0=ALU.mult,
+                op1=ALU.mult,
+            )
+
+        def cluster_probs(s):
+            j = units[s][1]
+            nc.gpsimd.tensor_scalar(
+                out=cluster[:, :, j],
+                in0=ex[s][:, HEAD_OUT:NH],
+                scalar1=rs[s][:, 1:2],
+                scalar2=1.0,
+                op0=ALU.mult,
+                op1=ALU.mult,
+            )
+
+        def store(lo, hi):
+            nc.sync.dma_start(out=out_view[:, lo:hi], in_=outs[:, lo:hi])
+
+        def finish(s):
+            kind, j = units[s]
+            if kind == "h":
+                normalise(s, nc.gpsimd, 0, 1024)
+                normalise(s, nc.gpsimd, 1024, HEAD_OUT)
+                cluster_probs(s)
+                lo, hi = -(-ROW * j // 16) * 16, (ROW * j + HEAD_OUT) // 16 * 16
+            else:
+                cut = VSHARE[s] - (ROW * j + HEAD_OUT) % 8 if s in VSHARE else 1024
+                normalise(s, nc.vector if s in VSHARE else nc.gpsimd, 0, cut)
+                normalise(s, nc.gpsimd, cut, NT)
+                lo, hi = (ROW * j + HEAD_OUT) // 16 * 16, -(-ROW * (j + 1) // 16) * 16
+            store(lo, hi)
+
+        last = len(units) - 1
+        x_unit = {place["h", j]: j for j in range(TILES)}
+        h_unit = {place["t", j]: j for j in range(TILES)}
+
+        def step(name, s):
+            lead = PLAN[name][0]
+            if name[:3] in ("sum", "rec"):
+                u = s + lead
+                if 0 <= u < last - 1 and (u >= EARLY) == (name[-1] == "E"):
+                    if name[:3] == "sum":
+                        row_sum(u)
+                    else:
+                        row_recip(u)
+                        finish(u)
+                return
+            if name[0] == "h":
+                j = h_unit.get(s + lead)
+            else:
+                j = x_unit.get(s + lead)
+            if j is None:
+                return
+            if name == "cast":
+                cast(j, {"v": nc.vector, "s": nc.scalar, "g": nc.gpsimd}[CAST[j]])
+            elif name == "xt":
+                x_transpose(j)
+            elif name == "p0":
+                x_product(j, 0)
+            elif name == "p1":
+                x_product(j, 1)
+            elif name == "xq":
+                x_quantize(j)
+            elif name == "hm":
+                h_matmul(j)
+            elif name == "hc":
+                h_copy(j)
+            elif name == "hq":
+                h_quantize(j)
+
+        anchors = ["e0", "m3", "x0", "e1", "m0", "x1", "e2", "m1", "x2", "e3", "m2", "x3", "ng"]
+
+        def anchor(a, s):
+            if a[0] == "e" and 0 <= s - 1 <= last:
+                bank_exp(s - 1, int(a[1]))
+            if a[0] == "m":
+                u = s if a[1] == "3" else s + 1
+                if 0 <= u <= last:
+                    logit_bank(u, int(a[1]))
+            if a[0] == "x" and 0 <= s <= last:
+                bank_max(s, int(a[1]))
+            if a == "ng" and 0 <= s <= last:
+                neg_max(s)
+
+        for s in range(-4, last + 4):
+            for i, a in enumerate(anchors):
+                anchor(a, s)
+                for name in NAMES:
+                    if PLAN[name][1] == i:
+                        step(name, s)
+
+        row_sum(last - 1)
+        row_recip(last - 1)
+        finish(last - 1)
+        nc.sync.dma_start(out=other_view, in_=cluster[:, 1, :])
+        row_sum(last)
+        row_recip(last)
+        base = ROW * (TILES - 1) + HEAD_OUT
+        normalise(last, nc.vector, 0, 1024)
+        normalise(last, nc.gpsimd, 1024, 1536)
+        tail_scale = stat.tile([P, 1], F32)
+        nc.vector.tensor_tensor(out=tail_scale[:], in0=rs[last][:, 1:2], in1=cluster[:, 0, TILES - 1 : TILES], op=ALU.mult)
+        nc.scalar.activation(outs[:, base + 1536 : base + NT], ex[last][:, 1536:NT], ACT.Copy, scale=tail_scale[:])
+        store(base, base + 1024)
+        store(base + 1024, TILES * ROW)

@@ -26,10 +26,13 @@ BANK = 512
 NB = NH // BANK
 LEAD = 4
 
-NAMES = ["cast", "xt", "p0", "p1", "xq", "hm", "hc", "hq", "sum", "recip", "sumE", "recE"]
-PLAN = {"cast": (4, 9), "xt": (2, 1), "p0": (2, 11), "p1": (1, 0), "xq": (1, 3), "hm": (2, 0), "hc": (2, 10), "hq": (1, 2), "sum": (-2, 0), "recip": (-2, 3), "sumE": (-1, 12), "recE": (-2, 4)}
+NAMES = ["cast", "xt", "p0", "p1", "xq", "hm", "hc", "hq", "sum", "recip", "sumE", "recE", "fin", "finE"]
+PLAN = {"cast": (4, 11), "xt": (2, 3), "p0": (2, 11), "p1": (1, 1), "xq": (1, 3), "hm": (2, 3), "hc": (2, 10), "hq": (1, 3), "sum": (-1, 11), "recip": (-2, 2), "sumE": (-2, 2), "recE": (-2, 4), "fin": (-2, 5), "finE": (-2, 4)}
 CAST = "vsssssss"
 EARLY = 12
+CHUNK = 2048
+SH = 0
+SUM_S = 0
 VSHARE = {13: 1024, 14: 1024}
 G = D // 512
 
@@ -257,7 +260,11 @@ def tile_adaptiveinputsoftmax_pa_w8_kernel(
         def row_sum(s):
             t = stat.tile([P, 2], F32, name="rs")
             rs[s] = t
-            nc.vector.tensor_reduce(out=t[:, 0:1], in_=sm[s][:], axis=AX.X, op=ALU.add)
+            if SUM_S:
+                junk = stat.tile([P, NB], F32, name="junk")
+                nc.scalar.activation(junk[:], sm[s][:], ACT.Copy, accum_out=t[:, 0:1])
+            else:
+                nc.vector.tensor_reduce(out=t[:, 0:1], in_=sm[s][:], axis=AX.X, op=ALU.add)
 
         def row_recip(s):
             nc.vector.reciprocal(out=rs[s][:, 1:2], in_=rs[s][:, 0:1])
@@ -273,6 +280,11 @@ def tile_adaptiveinputsoftmax_pa_w8_kernel(
                 op0=ALU.mult,
                 op1=ALU.mult,
             )
+
+        def pieces(s, eng, lo, hi):
+            while lo < hi:
+                normalise(s, eng, lo, min(lo + CHUNK, hi))
+                lo += CHUNK
 
         def cluster_probs(s):
             j = units[s][1]
@@ -291,14 +303,21 @@ def tile_adaptiveinputsoftmax_pa_w8_kernel(
         def finish(s):
             kind, j = units[s]
             if kind == "h":
-                normalise(s, nc.gpsimd, 0, 1024)
-                normalise(s, nc.gpsimd, 1024, HEAD_OUT)
+                pieces(s, nc.gpsimd, 0, HEAD_OUT - SH)
                 cluster_probs(s)
+                if SH:
+                    nc.scalar.activation(
+                        outs[:, ROW * j + HEAD_OUT - SH : ROW * j + HEAD_OUT],
+                        ex[s][:, HEAD_OUT - SH : HEAD_OUT],
+                        ACT.Copy,
+                        scale=rs[s][:, 1:2],
+                    )
                 lo, hi = -(-ROW * j // 16) * 16, (ROW * j + HEAD_OUT) // 16 * 16
             else:
-                cut = VSHARE[s] - (ROW * j + HEAD_OUT) % 8 if s in VSHARE else 1024
-                normalise(s, nc.vector if s in VSHARE else nc.gpsimd, 0, cut)
-                normalise(s, nc.gpsimd, cut, NT)
+                cut = VSHARE[s] - (ROW * j + HEAD_OUT) % 8 if s in VSHARE else 0
+                if cut:
+                    normalise(s, nc.vector, 0, cut)
+                pieces(s, nc.gpsimd, cut, NT)
                 lo, hi = (ROW * j + HEAD_OUT) // 16 * 16, -(-ROW * (j + 1) // 16) * 16
             store(lo, hi)
 
@@ -308,13 +327,14 @@ def tile_adaptiveinputsoftmax_pa_w8_kernel(
 
         def step(name, s):
             lead = PLAN[name][0]
-            if name[:3] in ("sum", "rec"):
+            if name[:3] in ("sum", "rec", "fin"):
                 u = s + lead
                 if 0 <= u < last - 1 and (u >= EARLY) == (name[-1] == "E"):
                     if name[:3] == "sum":
                         row_sum(u)
-                    else:
+                    elif name[:3] == "rec":
                         row_recip(u)
+                    else:
                         finish(u)
                 return
             if name[0] == "h":

@@ -68,6 +68,7 @@ def tile_adaptiveinputsoftmax_pa_w8_kernel(
         outs = keep.tile([P, TILES * ROW], F32, align_bytes=64)
         cluster = keep.tile([P, 2, TILES], F32)
         warm = keep.tile([P, 1], F32)
+        zero = keep.tile([P, BANK], BF16)
 
         x_view = x_bytes.flatten_outer_dims().rearrange("(p j) k -> p j k", j=TILES)
         out_view = probs.flatten_outer_dims().rearrange("(p j) c -> p (j c)", j=TILES)
@@ -79,10 +80,10 @@ def tile_adaptiveinputsoftmax_pa_w8_kernel(
         ctx.enter_context(tc.manual_schedule())
 
         nc.vector.memset(hs[:].bitcast(I32), 0)
+        nc.vector.memset(zero[:], 0.0)
         nc.vector.memset(warm[:], 0.0)
         nc.vector.memset(tws[:].bitcast(I32), 0)
         nc.vector.memset(tps[:].bitcast(I32), 0)
-        nc.scalar.activation(warm[:], warm[:], ACT.Exp)
         make_identity(nc, ident[:])
 
         def load_x(lo, hi):
@@ -94,8 +95,9 @@ def tile_adaptiveinputsoftmax_pa_w8_kernel(
             )
 
         load_x(0, 1)
-        nc.sync.dma_start(out=xs[:], in_=x_scale.rearrange("a b (g p t) -> p (a b g) t", g=G, p=P, t=4))
-        load_x(1, 2)
+        nc.scalar.dma_start(out=xs[:], in_=x_scale.rearrange("a b (g p t) -> p (a b g) t", g=G, p=P, t=4))
+        nc.scalar.dma_start(out=xb[:, 1, :], in_=x_view[:, 1, :])
+        nc.scalar.activation(warm[:], warm[:], ACT.Exp)
         for q in range(4):
             nc.sync.dma_start(
                 out=hs[32 * q : 32 * q + 8, :].bitcast(I32), in_=hw_scales[:, 4 * q : 4 * q + 4, :].bitcast(I32)
@@ -127,6 +129,13 @@ def tile_adaptiveinputsoftmax_pa_w8_kernel(
                 out=tpw_perm[:, g, :].rearrange("p (t m) -> p t m", t=4),
                 in_=tpw[:, g, :].rearrange("p (m t) -> p t m", t=4),
             )
+
+        def warm_up(n):
+            t = logits.tile([P, BANK], F32, name="lg")
+            for k in range(n):
+                nc.tensor.matmul(t[:], lhsT=zero[:, 0:P], rhs=zero[:], start=True, stop=True)
+
+        warm_up(4)
 
         xbf, xt, xg, xc, xsc = {}, {}, {}, {}, {}
         ht, hg, hc, hsc = {}, {}, {}, {}
@@ -347,6 +356,8 @@ def tile_adaptiveinputsoftmax_pa_w8_kernel(
                 cast(j, {"v": nc.vector, "s": nc.scalar, "g": nc.gpsimd}[CAST[j]])
             elif name == "xt":
                 x_transpose(j)
+                if j < 2:
+                    warm_up(2 - j)
             elif name == "p0":
                 x_product(j, 0)
             elif name == "p1":

from contextlib import ExitStack

import concourse.mybir as mybir
from concourse.masks import make_identity

F32 = mybir.dt.float32
BF16 = mybir.dt.bfloat16
I32 = mybir.dt.int32
U8 = mybir.dt.uint8
FP8 = mybir.dt.float8_e4m3fn
FP8X4 = mybir.dt.float8_e4m3fn_x4
ALU = mybir.AluOpType
ACT = mybir.ActivationFunctionType
AX = mybir.AxisListType

P = 128
NTOK = 1024
D = 1024
NH = 2048
HEAD_OUT = 2046
PROJ = 512
NT = 2048
ROW = HEAD_OUT + NT
TILES = NTOK // P
BANK = 512
NB = NH // BANK
LEAD = 4

NAMES = ["cast", "xt", "p0", "p1", "xq", "hm", "hc", "hq", "sum", "recip", "sumE", "recE", "fin", "finE"]
PLAN = {"cast": (4, 11), "xt": (2, 3), "p0": (2, 11), "p1": (1, 1), "xq": (1, 3), "hm": (2, 3), "hc": (2, 10), "hq": (1, 3), "sum": (-1, 11), "recip": (-2, 2), "sumE": (-2, 2), "recE": (-2, 4), "fin": (-2, 5), "finE": (-2, 4)}
CAST = "vsssssss"
EARLY = 12
CHUNK = 2048
SH = 0
SUM_S = 0
VSHARE = {13: 1024, 14: 1024}
G = D // 512

FLOPS = 2 * NTOK * (D * NH + D * PROJ + PROJ * NT)


def tile_adaptiveinputsoftmax_pa_w8_kernel(
    tc, x_bytes, x_scale, hw_words, hw_scales, tp_words, tp_scales, tw_words, tw_scales, probs, other
):
    nc = tc.nc

    with ExitStack() as ctx:
        keep = ctx.enter_context(tc.tile_pool(name="keep", bufs=1))
        work = ctx.enter_context(tc.tile_pool(name="work", bufs=2))
        work3 = ctx.enter_context(tc.tile_pool(name="work3", bufs=3))
        work5 = ctx.enter_context(tc.tile_pool(name="work5", bufs=5))
        epool = ctx.enter_context(tc.tile_pool(name="epool", bufs=4))
        stat = ctx.enter_context(tc.tile_pool(name="stat", bufs=5))
        logits = ctx.enter_context(tc.psum_pool(name="logits", bufs=7))
        misc = ctx.enter_context(tc.psum_pool(name="misc", bufs=1))

        xb = keep.tile([P, TILES, D], U8, align_bytes=64)
        xs = keep.tile([P, G, 4], F32)
        hw = keep.tile([P, NB, G, BANK], I32, align_bytes=64)
        hs = keep.tile([P, NH], U8, align_bytes=64)
        tpw = keep.tile([P, G, PROJ], I32, align_bytes=64)
        tps = keep.tile([P, PROJ], U8, align_bytes=64)
        tpw_perm = keep.tile([P, G, PROJ], I32, align_bytes=64)
        tps_perm = keep.tile([P, PROJ], U8, align_bytes=64)
        tw = keep.tile([P, NT], I32, align_bytes=64)
        tws = keep.tile([P, NT], U8, align_bytes=64)
        ident = keep.tile([P, P], F32)
        outs = keep.tile([P, TILES * ROW], F32, align_bytes=64)
        cluster = keep.tile([P, 2, TILES], F32)
        warm = keep.tile([P, 1], F32)
        zero = keep.tile([P, BANK], BF16)

        x_view = x_bytes.flatten_outer_dims().rearrange("(p j) k -> p j k", j=TILES)
        out_view = probs.flatten_outer_dims().rearrange("(p j) c -> p (j c)", j=TILES)
        other_view = other.flatten_outer_dims().rearrange("(p j) c -> p (j c)", j=TILES)
        hw_view = hw_words.rearrange("g p n t -> g p (n t)").bitcast(I32)
        tp_view = tp_words.rearrange("g p n t -> g p (n t)").bitcast(I32)
        tw_view = tw_words.rearrange("g p n t -> g p (n t)").bitcast(I32)

        ctx.enter_context(tc.manual_schedule())

        nc.vector.memset(hs[:].bitcast(I32), 0)
        nc.vector.memset(zero[:], 0.0)
        nc.vector.memset(warm[:], 0.0)
        nc.vector.memset(tws[:].bitcast(I32), 0)
        nc.vector.memset(tps[:].bitcast(I32), 0)
        make_identity(nc, ident[:])

        def load_x(lo, hi):
            nc.sync.dma_start(out=xb[:, lo:hi, :], in_=x_view[:, lo:hi, :])

        def load_head(b):
            nc.sync.dma_start(
                out=hw[:, b, :, :], in_=hw_view[:, :, BANK * b : BANK * (b + 1)].rearrange("g p n -> p g n")
            )

        load_x(0, 1)
        nc.scalar.dma_start(out=xs[:], in_=x_scale.rearrange("a b (g p t) -> p (a b g) t", g=G, p=P, t=4))
        nc.scalar.dma_start(out=xb[:, 1, :], in_=x_view[:, 1, :])
        nc.scalar.activation(warm[:], warm[:], ACT.Exp)
        for q in range(4):
            nc.sync.dma_start(
                out=hs[32 * q : 32 * q + 8, :].bitcast(I32), in_=hw_scales[:, 4 * q : 4 * q + 4, :].bitcast(I32)
            )
        load_head(0)
        load_head(1)
        load_x(2, 3)
        load_head(2)
        load_head(3)
        for q in range(4):
            nc.sync.dma_start(
                out=tps[32 * q : 32 * q + 8, :].bitcast(I32), in_=tp_scales[:, 4 * q : 4 * q + 4, :].bitcast(I32)
            )
        nc.sync.dma_start(out=tpw[:], in_=tp_view.rearrange("g p n -> p g n"))
        load_x(3, 4)
        for q in range(4):
            nc.sync.dma_start(
                out=tws[32 * q : 32 * q + 4, :].bitcast(I32), in_=tw_scales[0, 4 * q : 4 * q + 4, :].bitcast(I32)
            )
        nc.sync.dma_start(out=tw[:], in_=tw_view[0])
        load_x(4, 6)
        load_x(6, 8)

        nc.gpsimd.tensor_copy(
            out=tps_perm[:].rearrange("p (t m) -> p t m", t=4), in_=tps[:].rearrange("p (m t) -> p t m", t=4)
        )
        for g in range(G):
            nc.gpsimd.tensor_copy(
                out=tpw_perm[:, g, :].rearrange("p (t m) -> p t m", t=4),
                in_=tpw[:, g, :].rearrange("p (m t) -> p t m", t=4),
            )

        def warm_up(n):
            t = logits.tile([P, BANK], F32, name="lg")
            for k in range(n):
                nc.tensor.matmul(t[:], lhsT=zero[:, 0:P], rhs=zero[:], start=True, stop=True)

        warm_up(4)

        xbf, xt, xg, xc, xsc = {}, {}, {}, {}, {}
        ht, hg, hc, hsc = {}, {}, {}, {}
        lg, mx, nm, sm, rs, ex = {}, {}, {}, {}, {}, {}

        def cast(j, eng):
            src = xb[:, j, :].bitcast(FP8)
            t = work3.tile([P, D], BF16, name="xbf", align_bytes=64)
            xbf[j] = t
            if eng is nc.scalar:
                nc.scalar.copy(out=t[:], in_=src)
            else:
                eng.tensor_copy(out=t[:], in_=src)

        def x_transpose(j):
            t = misc.tile([P, BANK], F32, name="miscb")
            xt[j] = t
            words = xbf[j][:].bitcast(F32)
            for g in range(G):
                for u in range(2):
                    nc.tensor.transpose(
                        t[:, 128 * (2 * g + u) : 128 * (2 * g + u + 1)],
                        words[:, 256 * g + u : 256 * (g + 1) : 2],
                        ident[:],
                    )

        def x_product(j, g):
            if g == 0:
                t = work.tile([P, G, P, 4], BF16, name="xg", align_bytes=64)
                xg[j] = t
            nc.vector.tensor_tensor(
                out=xg[j][:, g, :, :].rearrange("p r (u e) -> p r u e", e=2),
                in0=xt[j][:, 256 * g : 256 * (g + 1)].bitcast(BF16).rearrange("p (u r e) -> p r u e", u=2, e=2),
                in1=xs[:, g, :].rearrange("p (u e) -> p u e", e=2).unsqueeze(1).to_broadcast([P, P, 2, 2]),
                op=ALU.mult,
            )

        def x_quantize(j):
            c = work5.tile([P, G * P], I32, name="xc", align_bytes=64)
            s = work5.tile([P, G * P], U8, name="xsc", align_bytes=64)
            xc[j], xsc[j] = c, s
            nc.vector.quantize_mx(
                out=c[:].bitcast(FP8X4), scales=s[:], in_=xg[j][:].rearrange("p g r t -> p (g r t)")
            )

        def h_matmul(j):
            t = misc.tile([P, BANK], F32, name="miscb")
            ht[j] = t
            for q in range(4):
                for g in range(G):
                    nc.tensor.matmul_mx(
                        out=t[:, P * q : P * (q + 1)],
                        lhsT=tpw_perm[:, g, P * q : P * (q + 1)].bitcast(FP8X4),
                        lhsT_scale=tps_perm[4 * g :, P * q : P * (q + 1)],
                        rhs=xc[j][:, P * g : P * (g + 1)].bitcast(FP8X4),
                        rhs_scale=xsc[j][:, P * g : P * (g + 1)],
                        start=(g == 0),
                        stop=(g == G - 1),
                    )

        def h_copy(j):
            t = work.tile([P, P, 4], BF16, name="hg", align_bytes=64)
            hg[j] = t
            nc.scalar.copy(out=t[:], in_=ht[j][:].rearrange("p (t n) -> p n t", t=4))

        def h_quantize(j):
            c = work3.tile([P, P], I32, name="hc", align_bytes=64)
            s = work3.tile([P, P], U8, name="hsc", align_bytes=64)
            hc[j], hsc[j] = c, s
            nc.vector.quantize_mx(out=c[:].bitcast(FP8X4), scales=s[:], in_=hg[j][:].rearrange("p n t -> p (n t)"))

        units = [("h", j) for j in range(LEAD)]
        for j in range(LEAD, TILES):
            units += [("t", j - LEAD), ("h", j)]
        units += [("t", j) for j in range(TILES - LEAD, TILES)]
        place = {unit: s for s, unit in enumerate(units)}

        def logit_bank(s, b):
            kind, j = units[s]
            t = logits.tile([P, BANK], F32, name="lg")
            lg[s, b] = t
            cols = slice(BANK * b, BANK * (b + 1))
            if kind == "h":
                for g in range(G):
                    nc.tensor.matmul_mx(
                        out=t[:],
                        lhsT=xc[j][:, P * g : P * (g + 1)].bitcast(FP8X4),
                        lhsT_scale=xsc[j][:, P * g : P * (g + 1)],
                        rhs=hw[:, b, g, :].bitcast(FP8X4),
                        rhs_scale=hs[4 * g :, cols],
                        start=(g == 0),
                        stop=(g == G - 1),
                    )
            else:
                nc.tensor.matmul_mx(
                    out=t[:],
                    lhsT=hc[j][:].bitcast(FP8X4),
                    lhsT_scale=hsc[j][:],
                    rhs=tw[:, cols].bitcast(FP8X4),
                    rhs_scale=tws[:, cols],
                    start=True,
                    stop=True,
                )

        def bank_max(s, b):
            if b == 0:
                t = stat.tile([P, NB], F32, name="mx")
                mx[s] = t
            nc.vector.tensor_reduce(out=mx[s][:, b : b + 1], in_=lg[s, b][:], axis=AX.X, op=ALU.max)

        def neg_max(s):
            t = stat.tile([P, 1], F32, name="nm")
            nm[s] = t
            nc.vector.tensor_reduce(out=t[:], in_=mx[s][:], axis=AX.X, op=ALU.max, negate=True)

        def bank_exp(s, b):
            if b == 0:
                t = stat.tile([P, NB], F32, name="sm")
                sm[s] = t
                e = epool.tile([P, NH], F32, name="ex", align_bytes=64)
                ex[s] = e
            nc.scalar.activation(
                ex[s][:, BANK * b : BANK * (b + 1)],
                lg[s, b][:],
                ACT.Exp,
                bias=nm[s][:],
                scale=1.0,
                accum_out=sm[s][:, b : b + 1],
            )

        def row_sum(s):
            t = stat.tile([P, 2], F32, name="rs")
            rs[s] = t
            if SUM_S:
                junk = stat.tile([P, NB], F32, name="junk")
                nc.scalar.activation(junk[:], sm[s][:], ACT.Copy, accum_out=t[:, 0:1])
            else:
                nc.vector.tensor_reduce(out=t[:, 0:1], in_=sm[s][:], axis=AX.X, op=ALU.add)

        def row_recip(s):
            nc.vector.reciprocal(out=rs[s][:, 1:2], in_=rs[s][:, 0:1])

        def normalise(s, eng, lo, hi):
            kind, j = units[s]
            base = ROW * j + (0 if kind == "h" else HEAD_OUT)
            eng.tensor_scalar(
                out=outs[:, base + lo : base + hi],
                in0=ex[s][:, lo:hi],
                scalar1=rs[s][:, 1:2],
                scalar2=1.0 if kind == "h" else cluster[:, 0, j : j + 1],
                op0=ALU.mult,
                op1=ALU.mult,
            )

        def pieces(s, eng, lo, hi):
            while lo < hi:
                normalise(s, eng, lo, min(lo + CHUNK, hi))
                lo += CHUNK

        def cluster_probs(s):
            j = units[s][1]
            nc.gpsimd.tensor_scalar(
                out=cluster[:, :, j],
                in0=ex[s][:, HEAD_OUT:NH],
                scalar1=rs[s][:, 1:2],
                scalar2=1.0,
                op0=ALU.mult,
                op1=ALU.mult,
            )

        def store(lo, hi):
            nc.sync.dma_start(out=out_view[:, lo:hi], in_=outs[:, lo:hi])

        def finish(s):
            kind, j = units[s]
            if kind == "h":
                pieces(s, nc.gpsimd, 0, HEAD_OUT - SH)
                cluster_probs(s)
                if SH:
                    nc.scalar.activation(
                        outs[:, ROW * j + HEAD_OUT - SH : ROW * j + HEAD_OUT],
                        ex[s][:, HEAD_OUT - SH : HEAD_OUT],
                        ACT.Copy,
                        scale=rs[s][:, 1:2],
                    )
                lo, hi = -(-ROW * j // 16) * 16, (ROW * j + HEAD_OUT) // 16 * 16
            else:
                cut = VSHARE[s] - (ROW * j + HEAD_OUT) % 8 if s in VSHARE else 0
                if cut:
                    normalise(s, nc.vector, 0, cut)
                pieces(s, nc.gpsimd, cut, NT)
                lo, hi = (ROW * j + HEAD_OUT) // 16 * 16, -(-ROW * (j + 1) // 16) * 16
            store(lo, hi)

        last = len(units) - 1
        x_unit = {place["h", j]: j for j in range(TILES)}
        h_unit = {place["t", j]: j for j in range(TILES)}

        def step(name, s):
            lead = PLAN[name][0]
            if name[:3] in ("sum", "rec", "fin"):
                u = s + lead
                if 0 <= u < last - 1 and (u >= EARLY) == (name[-1] == "E"):
                    if name[:3] == "sum":
                        row_sum(u)
                    elif name[:3] == "rec":
                        row_recip(u)
                    else:
                        finish(u)
                return
            if name[0] == "h":
                j = h_unit.get(s + lead)
            else:
                j = x_unit.get(s + lead)
            if j is None:
                return
            if name == "cast":
                cast(j, {"v": nc.vector, "s": nc.scalar, "g": nc.gpsimd}[CAST[j]])
            elif name == "xt":
                x_transpose(j)
                if j < 2:
                    warm_up(2 - j)
            elif name == "p0":
                x_product(j, 0)
            elif name == "p1":
                x_product(j, 1)
            elif name == "xq":
                x_quantize(j)
            elif name == "hm":
                h_matmul(j)
            elif name == "hc":
                h_copy(j)
            elif name == "hq":
                h_quantize(j)

        anchors = ["e0", "m3", "x0", "e1", "m0", "x1", "e2", "m1", "x2", "e3", "m2", "x3", "ng"]

        def anchor(a, s):
            if a[0] == "e" and 0 <= s - 1 <= last:
                bank_exp(s - 1, int(a[1]))
            if a[0] == "m":
                u = s if a[1] == "3" else s + 1
                if 0 <= u <= last:
                    logit_bank(u, int(a[1]))
            if a[0] == "x" and 0 <= s <= last:
                bank_max(s, int(a[1]))
            if a == "ng" and 0 <= s <= last:
                neg_max(s)

        for s in range(-4, last + 4):
            for i, a in enumerate(anchors):
                anchor(a, s)
                for name in NAMES:
                    if PLAN[name][1] == i:
                        step(name, s)

        row_sum(last - 1)
        row_recip(last - 1)
        finish(last - 1)
        nc.sync.dma_start(out=other_view, in_=cluster[:, 1, :])
        row_sum(last)
        row_recip(last)
        base = ROW * (TILES - 1) + HEAD_OUT
        normalise(last, nc.vector, 0, 1024)
        normalise(last, nc.gpsimd, 1024, 1536)
        tail_scale = stat.tile([P, 1], F32)
        nc.vector.tensor_tensor(out=tail_scale[:], in0=rs[last][:, 1:2], in1=cluster[:, 0, TILES - 1 : TILES], op=ALU.mult)
        nc.scalar.activation(outs[:, base + 1536 : base + NT], ex[last][:, 1536:NT], ACT.Copy, scale=tail_scale[:])
        store(base, base + 1024)
        store(base + 1024, TILES * ROW)
